import numpy as np
import ml_dtypes


def mxq(x, axis, fmt="e4m3"):
    dtype, down = {"e4m3": (ml_dtypes.float8_e4m3fn, 7), "e5m2": (ml_dtypes.float8_e5m2, 14)}[fmt]
    v = np.moveaxis(np.asarray(x, np.float32).astype(ml_dtypes.bfloat16).astype(np.float64), axis, -1)
    blocks = v.reshape(v.shape[:-1] + (-1, 32))
    amax = np.abs(blocks).max(-1, keepdims=True)
    byte = np.maximum(np.where(amax > 0, np.frexp(amax)[1] - 1 + 127, 0) - down, 1)
    scale = np.exp2(byte - 127.0)
    codes = (blocks / scale).astype(np.float32).astype(dtype).astype(np.float64)
    return np.moveaxis((codes * scale).reshape(v.shape), -1, axis)


WIDE = False


def mx_kscale(k):
    if not WIDE:
        return np.ones(k)
    levels = np.array([10, -10, 5, -5, 0])
    if k % 512:
        return np.exp2(np.random.permutation(np.resize(levels, k // 32))).repeat(32)
    a = np.empty((k // 512, 16))
    for p in range(k // 512):
        a[p, :8] = np.random.permutation(np.resize(levels, 8))
        for g in range(8):
            far = levels[np.abs(levels - a[p, g]) >= 10]
            a[p, g + 8] = far[np.random.randint(len(far))]
    return np.exp2(a.ravel()).repeat(32)


BF16 = ml_dtypes.bfloat16


def bf(x):
    return np.asarray(x, np.float32).astype(BF16)


def f64(x):
    return np.asarray(x).astype(np.float64)


E2M1 = np.array([0.0, 0.5, 1.0, 1.5, 2.0, 3.0, 4.0, 6.0, -0.0, -0.5, -1.0, -1.5, -2.0, -3.0, -4.0, -6.0])


def pack_weight(w, fmt):
    k, n = w.shape
    w = f64(bf(w)).reshape(k // 32, 32, n)
    amax = np.abs(w).max(1)
    if fmt == "e4m3":
        byte = np.frexp(amax)[1] - 1 + 127 - 7
    else:
        mant, ex = np.frexp(amax / 6.0)
        byte = np.where(mant > 0.5, ex, ex - 1) + 127
    byte = np.clip(np.where(amax > 0, byte, 1), 1, 254)
    scaled = (w * np.exp2(127.0 - byte)[:, None, :]).reshape(k, n).astype(np.float32)
    by_word = np.ascontiguousarray(scaled.reshape(k // 512, 128, 4, n).transpose(0, 1, 3, 2))
    if fmt == "e4m3":
        words = by_word.astype(ml_dtypes.float8_e4m3fn).view(np.uint8)
    else:
        c = by_word.astype(ml_dtypes.float4_e2m1fn).view(np.uint8) & 0xF
        words = c[..., 0::2] | (c[..., 1::2] << 4)
    return np.ascontiguousarray(words), np.ascontiguousarray(byte.astype(np.uint8).reshape(k // 512, 16, n))


def unpack_weight(words, scales, fmt):
    g, p, n, _ = words.shape
    if fmt == "e4m3":
        vals = np.ascontiguousarray(words).view(ml_dtypes.float8_e4m3fn).astype(np.float64)
    else:
        nib = np.empty((g, p, n, 4), np.uint8)
        nib[..., 0::2] = words & 0xF
        nib[..., 1::2] = words >> 4
        vals = E2M1[nib]
    vals = vals * np.repeat(np.exp2(scales.astype(np.float64) - 127.0), 8, axis=1)[..., None]
    return vals.transpose(0, 1, 3, 2).reshape(g * 512, n)


B, S, D, DFF, R = 4, 2048, 512, 1024, 512


def draw0():
    t, r = mx_kscale(DFF), mx_kscale(R)
    v = np.random.standard_normal((B, S, DFF)) * 1.2
    c_proj_U = bf(np.random.standard_normal((DFF, R)) * 2.0 / np.sqrt(DFF) / t[:, None])
    c_proj_S = bf(np.random.uniform(size=R) * r)
    words, scales = pack_weight((np.random.standard_normal((D, R)) / np.sqrt(R) / r[None, :]).T, "e4m3")
    return {"h_gelu": bf(v / (1.0 + np.exp(-1.702 * v)) * t),
            "c_proj_U": c_proj_U,
            "c_proj_S": c_proj_S,
            "c_proj_V_words": words,
            "c_proj_V_scales": scales,
            "c_proj_bias": bf(np.random.standard_normal(D) * 0.3)}


def core(h_gelu, c_proj_U, c_proj_S, c_proj_V_words, c_proj_V_scales, c_proj_bias):
    us = f64(c_proj_U) * f64(c_proj_S)[None, :]
    w = mxq(us, 1, "e4m3") @ unpack_weight(c_proj_V_words, c_proj_V_scales, "e4m3")
    return (mxq(f64(h_gelu), 2, "e4m3") @ mxq(w, 0, "e4m3")) + f64(c_proj_bias)


def e4m3fn_bytes(y):
    return np.clip(np.asarray(y, np.float64), -448.0, 448.0).astype(np.float32).astype(ml_dtypes.float8_e4m3fn).view(np.uint8)


def e4m3fn_values(b):
    return np.asarray(b, np.uint8).view(ml_dtypes.float8_e4m3fn).astype(np.float64)


def setup_inputs():
    d = draw0()
    x0 = np.asarray(d['h_gelu']).astype(np.float64)
    s = (np.max(np.abs(x0), axis=(0, 1), keepdims=True) / 448.0).astype(np.float32)
    out = {}
    for k, v in d.items():
        if k == 'h_gelu':
            out['h_gelu_bytes'] = e4m3fn_bytes(x0 / s.astype(np.float64))
            out['h_gelu_scale'] = s
        else:
            out[k] = v
    return out


def reference(h_gelu_bytes, h_gelu_scale, c_proj_U, c_proj_S, c_proj_V_words, c_proj_V_scales, c_proj_bias):
    return core(e4m3fn_values(h_gelu_bytes) * h_gelu_scale.astype(np.float64), c_proj_U, c_proj_S, c_proj_V_words, c_proj_V_scales, c_proj_bias)

@@ -1,0 +1,231 @@
+from contextlib import ExitStack
+
+import concourse.mybir as mybir
+from concourse.masks import make_identity
+
+B, S, D, DFF, R = 4, 2048, 512, 1024, 512
+FLOPS = 2 * B * S * DFF * D + 2 * DFF * R * D
+
+F32 = mybir.dt.float32
+BF16 = mybir.dt.bfloat16
+U32 = mybir.dt.uint32
+I32 = mybir.dt.int32
+U8 = mybir.dt.uint8
+E4M3 = mybir.dt.float8_e4m3fn
+X4 = mybir.dt.float8_e4m3fn_x4
+MULT = mybir.AluOpType.mult
+ADD = mybir.AluOpType.add
+
+P = 128
+GROUPS = B * S // (4 * P)
+PAIRS = 2 * GROUPS
+LAG = 3
+G_CHUNK = 256
+
+
+def tile_hybridsuperlayer_pb_t_w8_kernel(
+    tc, h_bytes, h_scale, c_proj_U, c_proj_S, c_proj_V_words, c_proj_V_scales, c_proj_bias, out
+):
+    nc = tc.nc
+    h_rows = h_bytes.rearrange("b s k -> (b s) k").rearrange("(n p j) k -> n p j k", p=P, j=4)
+    out_rows = out.rearrange("b s d -> (b s) d").rearrange("(n p j) d -> n p j d", p=P, j=4)
+    u_rows = c_proj_U.rearrange("(g m t) r -> g m t r", g=2, t=4)
+
+    with ExitStack() as ctx:
+        const = ctx.enter_context(tc.tile_pool(name="const", bufs=1))
+        stage = ctx.enter_context(tc.tile_pool(name="stage", bufs=3))
+        codes_pool = ctx.enter_context(tc.tile_pool(name="codes", bufs=LAG + 3))
+        psum = ctx.enter_context(tc.psum_pool(name="psum", bufs=2))
+
+        ident = const.tile([P, P], F32, name="ident")
+        make_identity(nc, ident[:])
+        v_scales = const.tile([P, D], U8, name="v_scales", align_bytes=64)
+        nc.vector.memset(v_scales[:].bitcast(I32), 0)
+
+        s_all = const.tile([P, R], BF16, name="s_all")
+        u_sb = const.tile([P, 2, 4, R], BF16, name="u_sb")
+        us = const.tile([P, 2, 4, R], BF16, name="us")
+        us_grouped = const.tile([P, 2, 4, P, 4], BF16, name="us_grouped", align_bytes=64)
+        us_codes = const.tile([P, 2, 4 * P], U32, name="us_codes", align_bytes=64)
+        us_scales = const.tile([P, 2, 4 * P], U8, name="us_scales", align_bytes=64)
+        v_words = const.tile([P, 4 * D], U8, name="v_words", align_bytes=64)
+        p_grouped = const.tile([P, 2, D, 4], BF16, name="p_grouped", align_bytes=64)
+        p_codes = const.tile([P, 2, D], U32, name="p_codes", align_bytes=64)
+        p_scales = const.tile([P, 2, D], U8, name="p_scales", align_bytes=64)
+        scale_col = const.tile([P, 2, 4], F32, name="scale_col")
+        scale_row = const.tile([P, DFF], F32, name="scale_row")
+        bias_all = const.tile([P, D], BF16, name="bias_all")
+
+        byte_tiles = {}
+        wide_tiles = {}
+        prod_tiles = {}
+        grouped_tiles = {}
+        code_tiles = {}
+        even_banks = {}
+        odd_banks = {}
+        out_banks = {}
+
+        def load(n):
+            raw = stage.tile([P, 4, DFF], U8, name="raw", tag="raw", bufs=4)
+            nc.sync.dma_start(out=raw[:], in_=h_rows[n])
+            byte_tiles[n] = raw
+
+        def cast(i):
+            raw = byte_tiles[i // 2]
+            j = 2 * (i % 2)
+            wide = stage.tile([P, 2, DFF], BF16, name="wide", tag="wide", bufs=5)
+            nc.scalar.copy(out=wide[:], in_=raw[:, j : j + 2, :].bitcast(E4M3))
+            wide_tiles[i] = wide
+
+        def gprod(i):
+            prod = stage.tile([P, DFF], BF16, name="prod", tag="prod", bufs=4)
+            for c in range(0, DFF, G_CHUNK):
+                nc.gpsimd.tensor_tensor(
+                    out=prod[:, c : c + G_CHUNK], in0=wide_tiles[i][:, 1, c : c + G_CHUNK],
+                    in1=scale_row[:, c : c + G_CHUNK], op=MULT)
+            prod_tiles[i] = prod
+
+        def turn(bank, words):
+            for g in range(2):
+                for u in range(2):
+                    nc.tensor.transpose(bank[:, u, g, :], words[:, 256 * g + u : 256 * (g + 1) : 2], ident[:])
+
+        def transposes(i):
+            even = psum.tile([P, 2, 2, P], F32, name="even", tag="even")
+            turn(even, wide_tiles[i][:, 0, :].bitcast(F32))
+            odd = psum.tile([P, 2, 2, P], F32, name="odd", tag="odd")
+            turn(odd, prod_tiles[i][:].bitcast(F32))
+            even_banks[i] = even
+            odd_banks[i] = odd
+
+        def vprod(i):
+            grouped = stage.tile([P, 2, 2, P, 4], BF16, name="grouped", tag="grouped", align_bytes=64)
+            nc.vector.tensor_tensor(
+                out=grouped[:, 0, :, :, :].rearrange("p g r (u e) -> p g r u e", u=2),
+                in0=even_banks[i][:].bitcast(BF16).rearrange("p u g (r e) -> p g r u e", e=2),
+                in1=scale_col[:].rearrange("p g (u e) -> p g u e", u=2).unsqueeze(2).broadcast_to([P, 2, P, 2, 2]),
+                op=MULT)
+            grouped_tiles[i] = grouped
+
+        def sexit(i):
+            nc.scalar.copy(
+                out=grouped_tiles[i][:, 1, :, :, :].rearrange("p g r t -> p (g r t)").bitcast(F32).rearrange("p (x u) -> p x u", u=2),
+                in_=odd_banks[i][:].rearrange("p u g r -> p (g r) u"))
+
+        def quant(i):
+            codes = codes_pool.tile([P, 4, P], U32, name="codes", align_bytes=64)
+            scales = codes_pool.tile([P, 4, P], U8, name="scales", align_bytes=64)
+            nc.vector.quantize_mx(
+                out=codes[:].rearrange("p x r -> p (x r)").bitcast(X4),
+                scales=scales[:].rearrange("p x r -> p (x r)"),
+                in_=grouped_tiles[i][:].rearrange("p a g r t -> p (a g r t)"))
+            code_tiles[i] = (codes, scales)
+
+        def mx(i):
+            codes, scales = code_tiles[i]
+            for a in range(2):
+                bank = psum.tile([P, D], F32, name="acc", tag="acc", bufs=4)
+                for g in range(2):
+                    nc.tensor.matmul_mx(
+                        out=bank[:], lhsT=codes[:, 2 * a + g, :].bitcast(X4), lhsT_scale=scales[:, 2 * a + g, :],
+                        rhs=p_codes[:, g, :].bitcast(X4), rhs_scale=p_scales[:, g, :],
+                        start=(g == 0), stop=(g == 1))
+                out_banks[i, a] = bank
+
+        def finish(i):
+            res = stage.tile([P, 2, D], F32, name="res", tag="res", bufs=4)
+            for a in range(2):
+                nc.vector.tensor_tensor(out=res[:, a, :], in0=out_banks[i, a][:], in1=bias_all[:], op=ADD)
+            j = 2 * (i % 2)
+            nc.sync.dma_start(out=out_rows[i // 2][:, j : j + 2, :], in_=res[:])
+
+        def us_product(g):
+            nc.vector.tensor_tensor(out=us[:, g], in0=u_sb[:, g], in1=s_all[:].unsqueeze(1).broadcast_to([P, 4, R]), op=MULT)
+
+        def us_turn(g):
+            for t0 in (0, 2):
+                bank = psum.tile([P, 2, 2, P], F32, name="acc", tag="acc", bufs=4)
+                for a in range(2):
+                    words = us[:, g, t0 + a, :].bitcast(F32)
+                    for u in range(2):
+                        nc.tensor.transpose(bank[:, a, u, :], words[:, u : 256 : 2], ident[:])
+                nc.scalar.copy(
+                    out=us_grouped[:, g, t0 : t0 + 2, :, :].rearrange("p a m t -> p (a m t)").bitcast(F32).rearrange("p (a m u) -> p a m u", a=2, u=2),
+                    in_=bank[:].rearrange("p a u m -> p a m u"))
+
+        def us_quant(g):
+            nc.vector.quantize_mx(
+                out=us_codes[:, g, :].bitcast(X4), scales=us_scales[:, g, :],
+                in_=us_grouped[:, g].rearrange("p t m x -> p (t m x)"))
+
+        def p_product(g):
+            for c in range(4):
+                bank = psum.tile([P, 4, P], F32, name="acc", tag="acc", bufs=4)
+                for t in range(4):
+                    nc.tensor.matmul_mx(
+                        out=bank[:, t, :], lhsT=us_codes[:, g, t * P : (t + 1) * P].bitcast(X4),
+                        lhsT_scale=us_scales[:, g, t * P : (t + 1) * P],
+                        rhs=v_words[:, 4 * P * c : 4 * P * (c + 1)].bitcast(X4),
+                        rhs_scale=v_scales[:, P * c : P * (c + 1)], start=True, stop=True)
+                copy = nc.scalar.copy if c % 2 == 0 else nc.vector.tensor_copy
+                copy(out=p_grouped[:, g, P * c : P * (c + 1), :], in_=bank[:].rearrange("p t n -> p n t"))
+
+        def p_quant(g):
+            nc.vector.quantize_mx(
+                out=p_codes[:, g, :].bitcast(X4), scales=p_scales[:, g, :],
+                in_=p_grouped[:, g].rearrange("p n t -> p (n t)"))
+
+        def step(i):
+            transposes(i)
+            vprod(i)
+            if i + 3 < PAIRS:
+                cast(i + 3)
+            sexit(i)
+            if i + 2 < PAIRS:
+                gprod(i + 2)
+
+        with tc.manual_schedule():
+            nc.sync.dma_start(out=s_all[:], in_=c_proj_S.partition_broadcast(P))
+            nc.sync.dma_start(out=u_sb[:, 0], in_=u_rows[0])
+            load(0)
+            nc.sync.dma_start(out=u_sb[:, 1], in_=u_rows[1])
+            nc.sync.dma_start(out=scale_row[:], in_=h_scale.rearrange("a o k -> (a o k)").partition_broadcast(P))
+            nc.sync.dma_start(out=scale_col[:], in_=h_scale.rearrange("a o (g p t) -> p (a o g) t", g=2, t=4))
+            nc.sync.dma_start(out=v_words[:].bitcast(I32), in_=c_proj_V_words[0].rearrange("p n t -> p (n t)").bitcast(I32))
+            for q in range(4):
+                nc.sync.dma_start(
+                    out=v_scales[32 * q : 32 * q + 4, :].bitcast(I32),
+                    in_=c_proj_V_scales[0, 4 * q : 4 * q + 4, :].bitcast(I32))
+            load(1)
+            nc.sync.dma_start(out=bias_all[:], in_=c_proj_bias.partition_broadcast(P))
+            load(2)
+
+            cast(0)
+            us_product(0)
+            us_product(1)
+            us_turn(0)
+            gprod(0)
+            us_turn(1)
+            us_quant(0)
+            cast(1)
+            us_quant(1)
+            gprod(1)
+            cast(2)
+            for i in range(PAIRS):
+                if i % 2 == 1 and (i + 5) // 2 < GROUPS:
+                    load((i + 5) // 2)
+                step(i)
+                if i == 0:
+                    p_product(0)
+                if i == 1:
+                    p_quant(0)
+                    p_product(1)
+                if i == 2:
+                    p_quant(1)
+                if i >= LAG:
+                    mx(i - LAG)
+                    finish(i - LAG)
+                quant(i)
+            for i in range(PAIRS - LAG, PAIRS):
+                mx(i)
+                finish(i)

@@ -20,7 +20,7 @@ P = 128
 GROUPS = B * S // (4 * P)
 PAIRS = 2 * GROUPS
 LAG = 3
-G_CHUNK = 256
+ADD_COLS = 256
 
 
 def tile_hybridsuperlayer_pb_t_w8_kernel(
@@ -53,16 +53,15 @@ def tile_hybridsuperlayer_pb_t_w8_kernel(
         p_codes = const.tile([P, 2, D], U32, name="p_codes", align_bytes=64)
         p_scales = const.tile([P, 2, D], U8, name="p_scales", align_bytes=64)
         scale_col = const.tile([P, 2, 4], F32, name="scale_col")
-        scale_row = const.tile([P, DFF], F32, name="scale_row")
         bias_all = const.tile([P, D], BF16, name="bias_all")
+        bias_f32 = const.tile([P, D], F32, name="bias_f32")
 
         byte_tiles = {}
         wide_tiles = {}
-        prod_tiles = {}
+        res_tiles = {}
         grouped_tiles = {}
         code_tiles = {}
-        even_banks = {}
-        odd_banks = {}
+        turned = {}
         out_banks = {}
 
         def load(n):
@@ -77,40 +76,26 @@ def tile_hybridsuperlayer_pb_t_w8_kernel(
             nc.scalar.copy(out=wide[:], in_=raw[:, j : j + 2, :].bitcast(E4M3))
             wide_tiles[i] = wide
 
-        def gprod(i):
-            prod = stage.tile([P, DFF], BF16, name="prod", tag="prod", bufs=4)
-            for c in range(0, DFF, G_CHUNK):
-                nc.gpsimd.tensor_tensor(
-                    out=prod[:, c : c + G_CHUNK], in0=wide_tiles[i][:, 1, c : c + G_CHUNK],
-                    in1=scale_row[:, c : c + G_CHUNK], op=MULT)
-            prod_tiles[i] = prod
-
         def turn(bank, words):
             for g in range(2):
                 for u in range(2):
                     nc.tensor.transpose(bank[:, u, g, :], words[:, 256 * g + u : 256 * (g + 1) : 2], ident[:])
 
         def transposes(i):
-            even = psum.tile([P, 2, 2, P], F32, name="even", tag="even")
-            turn(even, wide_tiles[i][:, 0, :].bitcast(F32))
-            odd = psum.tile([P, 2, 2, P], F32, name="odd", tag="odd")
-            turn(odd, prod_tiles[i][:].bitcast(F32))
-            even_banks[i] = even
-            odd_banks[i] = odd
+            for a in range(2):
+                bank = psum.tile([P, 2, 2, P], F32, name="turned_bank", tag="turned", bufs=4)
+                turn(bank, wide_tiles[i][:, a, :].bitcast(F32))
+                turned[i, a] = bank
 
         def vprod(i):
             grouped = stage.tile([P, 2, 2, P, 4], BF16, name="grouped", tag="grouped", align_bytes=64)
-            nc.vector.tensor_tensor(
-                out=grouped[:, 0, :, :, :].rearrange("p g r (u e) -> p g r u e", u=2),
-                in0=even_banks[i][:].bitcast(BF16).rearrange("p u g (r e) -> p g r u e", e=2),
-                in1=scale_col[:].rearrange("p g (u e) -> p g u e", u=2).unsqueeze(2).broadcast_to([P, 2, P, 2, 2]),
-                op=MULT)
+            for a in range(2):
+                nc.vector.tensor_tensor(
+                    out=grouped[:, a, :, :, :].rearrange("p g r (u e) -> p g r u e", u=2),
+                    in0=turned[i, a][:].bitcast(BF16).rearrange("p u g (r e) -> p g r u e", e=2),
+                    in1=scale_col[:].rearrange("p g (u e) -> p g u e", u=2).unsqueeze(2).broadcast_to([P, 2, P, 2, 2]),
+                    op=MULT)
             grouped_tiles[i] = grouped
-
-        def sexit(i):
-            nc.scalar.copy(
-                out=grouped_tiles[i][:, 1, :, :, :].rearrange("p g r t -> p (g r t)").bitcast(F32).rearrange("p (x u) -> p x u", u=2),
-                in_=odd_banks[i][:].rearrange("p u g r -> p (g r) u"))
 
         def quant(i):
             codes = codes_pool.tile([P, 4, P], U32, name="codes", align_bytes=64)
@@ -135,7 +120,16 @@ def tile_hybridsuperlayer_pb_t_w8_kernel(
         def finish(i):
             res = stage.tile([P, 2, D], F32, name="res", tag="res", bufs=4)
             for a in range(2):
-                nc.vector.tensor_tensor(out=res[:, a, :], in0=out_banks[i, a][:], in1=bias_all[:], op=ADD)
+                nc.scalar.copy(out=res[:, a, :], in_=out_banks[i, a][:])
+            res_tiles[i] = res
+
+        def add_bias(i):
+            res = res_tiles[i]
+            for a in range(2):
+                for c in range(0, D, ADD_COLS):
+                    nc.gpsimd.tensor_tensor(
+                        out=res[:, a, c : c + ADD_COLS], in0=res[:, a, c : c + ADD_COLS],
+                        in1=bias_f32[:, c : c + ADD_COLS], op=ADD)
             j = 2 * (i % 2)
             nc.sync.dma_start(out=out_rows[i // 2][:, j : j + 2, :], in_=res[:])
 
@@ -175,21 +169,11 @@ def tile_hybridsuperlayer_pb_t_w8_kernel(
                 out=p_codes[:, g, :].bitcast(X4), scales=p_scales[:, g, :],
                 in_=p_grouped[:, g].rearrange("p n t -> p (n t)"))
 
-        def step(i):
-            transposes(i)
-            vprod(i)
-            if i + 3 < PAIRS:
-                cast(i + 3)
-            sexit(i)
-            if i + 2 < PAIRS:
-                gprod(i + 2)
-
         with tc.manual_schedule():
             nc.sync.dma_start(out=s_all[:], in_=c_proj_S.partition_broadcast(P))
             nc.sync.dma_start(out=u_sb[:, 0], in_=u_rows[0])
             load(0)
             nc.sync.dma_start(out=u_sb[:, 1], in_=u_rows[1])
-            nc.sync.dma_start(out=scale_row[:], in_=h_scale.rearrange("a o k -> (a o k)").partition_broadcast(P))
             nc.sync.dma_start(out=scale_col[:], in_=h_scale.rearrange("a o (g p t) -> p (a o g) t", g=2, t=4))
             nc.sync.dma_start(out=v_words[:].bitcast(I32), in_=c_proj_V_words[0].rearrange("p n t -> p (n t)").bitcast(I32))
             for q in range(4):
@@ -204,17 +188,19 @@ def tile_hybridsuperlayer_pb_t_w8_kernel(
             us_product(0)
             us_product(1)
             us_turn(0)
-            gprod(0)
             us_turn(1)
             us_quant(0)
             cast(1)
             us_quant(1)
-            gprod(1)
+            nc.gpsimd.tensor_copy(out=bias_f32[:], in_=bias_all[:])
             cast(2)
             for i in range(PAIRS):
                 if i % 2 == 1 and (i + 5) // 2 < GROUPS:
                     load((i + 5) // 2)
-                step(i)
+                transposes(i)
+                vprod(i)
+                if i + 3 < PAIRS:
+                    cast(i + 3)
                 if i == 0:
                     p_product(0)
                 if i == 1:
@@ -225,7 +211,11 @@ def tile_hybridsuperlayer_pb_t_w8_kernel(
                 if i >= LAG:
                     mx(i - LAG)
                     finish(i - LAG)
-                quant(i)
+                    add_bias(i - LAG)
+                if i >= 1:
+                    quant(i - 1)
+            quant(PAIRS - 1)
             for i in range(PAIRS - LAG, PAIRS):
                 mx(i)
                 finish(i)
+                add_bias(i)

@@ -15,12 +15,17 @@ E4M3 = mybir.dt.float8_e4m3fn
 X4 = mybir.dt.float8_e4m3fn_x4
 MULT = mybir.AluOpType.mult
 ADD = mybir.AluOpType.add
+COPY = mybir.ActivationFunctionType.Copy
 
 P = 128
 GROUPS = B * S // (4 * P)
 PAIRS = 2 * GROUPS
-LAG = 3
-ADD_COLS = 256
+LM, LX, LW, LQ, LF, LC, LP = 5, 0, 1, 1, 5, 2, 1
+VORDER = ("p", "w", "f0", "f1", "q")
+SORDER = ("x0", "x1", "c")
+PEORDER = ("t0", "m0", "t1", "m1")
+P_ON_V = 2
+P_AT = 2
 
 
 def tile_hybridsuperlayer_pb_t_w8_kernel(
@@ -34,13 +39,13 @@ def tile_hybridsuperlayer_pb_t_w8_kernel(
     with ExitStack() as ctx:
         const = ctx.enter_context(tc.tile_pool(name="const", bufs=1))
         stage = ctx.enter_context(tc.tile_pool(name="stage", bufs=3))
-        codes_pool = ctx.enter_context(tc.tile_pool(name="codes", bufs=LAG + 3))
+        codes_pool = ctx.enter_context(tc.tile_pool(name="codes", bufs=LM + 3))
         psum = ctx.enter_context(tc.psum_pool(name="psum", bufs=2))
 
         ident = const.tile([P, P], F32, name="ident")
         make_identity(nc, ident[:])
         v_scales = const.tile([P, D], U8, name="v_scales", align_bytes=64)
-        nc.vector.memset(v_scales[:].bitcast(I32), 0)
+        nc.gpsimd.memset(v_scales[:].bitcast(I32), 0)
 
         s_all = const.tile([P, R], BF16, name="s_all")
         u_sb = const.tile([P, 2, 4, R], BF16, name="u_sb")
@@ -52,17 +57,20 @@ def tile_hybridsuperlayer_pb_t_w8_kernel(
         p_grouped = const.tile([P, 2, D, 4], BF16, name="p_grouped", align_bytes=64)
         p_codes = const.tile([P, 2, D], U32, name="p_codes", align_bytes=64)
         p_scales = const.tile([P, 2, D], U8, name="p_scales", align_bytes=64)
-        scale_col = const.tile([P, 2, 4], F32, name="scale_col")
+        scale_col = const.tile([P, 4], F32, name="scale_col")
+        scale_row = const.tile([P, 512], F32, name="scale_row")
         bias_all = const.tile([P, D], BF16, name="bias_all")
-        bias_f32 = const.tile([P, D], F32, name="bias_f32")
 
         byte_tiles = {}
         wide_tiles = {}
-        res_tiles = {}
+        prod_tiles = {}
+        banks0 = {}
+        banks1 = {}
+        pair_tiles = {}
         grouped_tiles = {}
         code_tiles = {}
-        turned = {}
         out_banks = {}
+        res_tiles = {}
 
         def load(n):
             raw = stage.tile([P, 4, DFF], U8, name="raw", tag="raw", bufs=4)
@@ -70,68 +78,79 @@ def tile_hybridsuperlayer_pb_t_w8_kernel(
             byte_tiles[n] = raw
 
         def cast(i):
-            raw = byte_tiles[i // 2]
-            j = 2 * (i % 2)
-            wide = stage.tile([P, 2, DFF], BF16, name="wide", tag="wide", bufs=5)
-            nc.scalar.copy(out=wide[:], in_=raw[:, j : j + 2, :].bitcast(E4M3))
+            wide = stage.tile([P, 2, 512], BF16, name="wide", tag="wide", bufs=LC + 2)
+            for a in range(2):
+                nc.scalar.copy(out=wide[:, a, :], in_=byte_tiles[i // 2][:, 2 * (i % 2) + a, 0:512].bitcast(E4M3))
             wide_tiles[i] = wide
 
-        def turn(bank, words):
-            for g in range(2):
-                for u in range(2):
-                    nc.tensor.transpose(bank[:, u, g, :], words[:, 256 * g + u : 256 * (g + 1) : 2], ident[:])
-
-        def transposes(i):
-            for a in range(2):
-                bank = psum.tile([P, 2, 2, P], F32, name="turned_bank", tag="turned", bufs=4)
-                turn(bank, wide_tiles[i][:, a, :].bitcast(F32))
-                turned[i, a] = bank
-
-        def vprod(i):
-            grouped = stage.tile([P, 2, 2, P, 4], BF16, name="grouped", tag="grouped", align_bytes=64)
+        def product(i):
+            prod = stage.tile([P, 2, 512], BF16, name="prod", tag="prod", bufs=LP + 2)
             for a in range(2):
                 nc.vector.tensor_tensor(
-                    out=grouped[:, a, :, :, :].rearrange("p g r (u e) -> p g r u e", u=2),
-                    in0=turned[i, a][:].bitcast(BF16).rearrange("p u g (r e) -> p g r u e", e=2),
-                    in1=scale_col[:].rearrange("p g (u e) -> p g u e", u=2).unsqueeze(2).broadcast_to([P, 2, P, 2, 2]),
-                    op=MULT)
+                    out=prod[:, a, :], in0=byte_tiles[i // 2][:, 2 * (i % 2) + a, 512:1024].bitcast(E4M3),
+                    in1=scale_row[:], op=MULT)
+            prod_tiles[i] = prod
+
+        def turn(rows, tag):
+            bank = psum.tile([P, 2, 2, P], F32, name=tag, tag=tag, bufs=2)
+            for a in range(2):
+                words = rows[:, a, :].bitcast(F32)
+                for u in range(2):
+                    nc.tensor.transpose(bank[:, u, a, :], words[:, u:256:2], ident[:])
+            return bank
+
+        def exit0(i):
+            pair = stage.tile([P, 2, 2 * P, 2], BF16, name="pair", tag="pair", bufs=4)
+            for u in range(2):
+                halves = banks0[i][:, u, :, :].rearrange("p a r -> p (a r)").bitcast(BF16).rearrange("p (x e) -> p x e", e=2)
+                for e in range(2):
+                    nc.scalar.activation(
+                        out=pair[:, u, :, e], in_=halves[:, :, e], func=COPY,
+                        scale=scale_col[:, 2 * u + e : 2 * u + e + 1])
+            pair_tiles[i] = pair
+
+        def exit1(i):
+            grouped = stage.tile([P, 2, 2 * P, 4], BF16, name="grouped", tag="grouped", bufs=5, align_bytes=64)
             grouped_tiles[i] = grouped
+            nc.scalar.copy(
+                out=grouped[:, 1, :, :].rearrange("p x t -> p (x t)").bitcast(F32).rearrange("p (x u) -> p x u", u=2),
+                in_=banks1[i][:].rearrange("p u a r -> p (a r) u"))
+
+        def weave(i):
+            nc.vector.tensor_copy(
+                out=grouped_tiles[i][:, 0, :, :].rearrange("p x t -> p (x t)").bitcast(F32).rearrange("p (x u) -> p x u", u=2),
+                in_=pair_tiles[i][:].rearrange("p u x e -> p (u x e)").bitcast(F32).rearrange("p (u x) -> p x u", u=2))
 
         def quant(i):
-            codes = codes_pool.tile([P, 4, P], U32, name="codes", align_bytes=64)
-            scales = codes_pool.tile([P, 4, P], U8, name="scales", align_bytes=64)
+            codes = codes_pool.tile([P, 2, 2 * P], U32, name="codes", align_bytes=64)
+            scales = codes_pool.tile([P, 2, 2 * P], U8, name="scales", align_bytes=64)
             nc.vector.quantize_mx(
-                out=codes[:].rearrange("p x r -> p (x r)").bitcast(X4),
-                scales=scales[:].rearrange("p x r -> p (x r)"),
-                in_=grouped_tiles[i][:].rearrange("p a g r t -> p (a g r t)"))
+                out=codes[:].rearrange("p g x -> p (g x)").bitcast(X4),
+                scales=scales[:].rearrange("p g x -> p (g x)"),
+                in_=grouped_tiles[i][:].rearrange("p g x t -> p (g x t)"))
             code_tiles[i] = (codes, scales)
 
-        def mx(i):
+        def mx(i, a):
             codes, scales = code_tiles[i]
-            for a in range(2):
-                bank = psum.tile([P, D], F32, name="acc", tag="acc", bufs=4)
-                for g in range(2):
-                    nc.tensor.matmul_mx(
-                        out=bank[:], lhsT=codes[:, 2 * a + g, :].bitcast(X4), lhsT_scale=scales[:, 2 * a + g, :],
-                        rhs=p_codes[:, g, :].bitcast(X4), rhs_scale=p_scales[:, g, :],
-                        start=(g == 0), stop=(g == 1))
-                out_banks[i, a] = bank
+            bank = psum.tile([P, D], F32, name="acc", tag="acc", bufs=4)
+            for g in range(2):
+                nc.tensor.matmul_mx(
+                    out=bank[:], lhsT=codes[:, g, P * a : P * (a + 1)].bitcast(X4), lhsT_scale=scales[:, g, P * a : P * (a + 1)],
+                    rhs=p_codes[:, g, :].bitcast(X4), rhs_scale=p_scales[:, g, :],
+                    start=(g == 0), stop=(g == 1))
+            out_banks[i, a] = bank
 
-        def finish(i):
-            res = stage.tile([P, 2, D], F32, name="res", tag="res", bufs=4)
-            for a in range(2):
-                nc.scalar.copy(out=res[:, a, :], in_=out_banks[i, a][:])
-            res_tiles[i] = res
-
-        def add_bias(i):
-            res = res_tiles[i]
-            for a in range(2):
-                for c in range(0, D, ADD_COLS):
-                    nc.gpsimd.tensor_tensor(
-                        out=res[:, a, c : c + ADD_COLS], in0=res[:, a, c : c + ADD_COLS],
-                        in1=bias_f32[:, c : c + ADD_COLS], op=ADD)
-            j = 2 * (i % 2)
-            nc.sync.dma_start(out=out_rows[i // 2][:, j : j + 2, :], in_=res[:])
+        def finish(i, a):
+            if a == 0:
+                res = stage.tile([P, 2, D], F32, name="res", tag="res", bufs=4)
+                res_tiles[i] = res
+            nc.vector.tensor_tensor(out=res_tiles[i][:, a, :], in0=out_banks[i, a][:], in1=bias_all[:], op=ADD)
+            if i == PAIRS - 1:
+                j = 2 * (i % 2) + a
+                nc.sync.dma_start(out=out_rows[i // 2][:, j, :], in_=res_tiles[i][:, a, :])
+            elif a == 1:
+                j = 2 * (i % 2)
+                nc.sync.dma_start(out=out_rows[i // 2][:, j : j + 2, :], in_=res_tiles[i][:])
 
         def us_product(g):
             nc.vector.tensor_tensor(out=us[:, g], in0=u_sb[:, g], in1=s_all[:].unsqueeze(1).broadcast_to([P, 4, R]), op=MULT)
@@ -161,7 +180,7 @@ def tile_hybridsuperlayer_pb_t_w8_kernel(
                         lhsT_scale=us_scales[:, g, t * P : (t + 1) * P],
                         rhs=v_words[:, 4 * P * c : 4 * P * (c + 1)].bitcast(X4),
                         rhs_scale=v_scales[:, P * c : P * (c + 1)], start=True, stop=True)
-                copy = nc.scalar.copy if c % 2 == 0 else nc.vector.tensor_copy
+                copy = nc.vector.tensor_copy if c < P_ON_V else nc.scalar.copy
                 copy(out=p_grouped[:, g, P * c : P * (c + 1), :], in_=bank[:].rearrange("p t n -> p n t"))
 
         def p_quant(g):
@@ -169,53 +188,70 @@ def tile_hybridsuperlayer_pb_t_w8_kernel(
                 out=p_codes[:, g, :].bitcast(X4), scales=p_scales[:, g, :],
                 in_=p_grouped[:, g].rearrange("p n t -> p (n t)"))
 
+        def ok(i):
+            return 0 <= i < PAIRS
+
         with tc.manual_schedule():
+            load(0)
+            nc.sync.dma_start(out=scale_row[:], in_=h_scale.rearrange("a o k -> (a o k)")[512:1024].partition_broadcast(P))
             nc.sync.dma_start(out=s_all[:], in_=c_proj_S.partition_broadcast(P))
             nc.sync.dma_start(out=u_sb[:, 0], in_=u_rows[0])
-            load(0)
+            nc.sync.dma_start(out=scale_col[:], in_=h_scale.rearrange("a o k -> (a o k)")[0:512].rearrange("(p t) -> p t", t=4))
             nc.sync.dma_start(out=u_sb[:, 1], in_=u_rows[1])
-            nc.sync.dma_start(out=scale_col[:], in_=h_scale.rearrange("a o (g p t) -> p (a o g) t", g=2, t=4))
+            load(1)
             nc.sync.dma_start(out=v_words[:].bitcast(I32), in_=c_proj_V_words[0].rearrange("p n t -> p (n t)").bitcast(I32))
             for q in range(4):
                 nc.sync.dma_start(
                     out=v_scales[32 * q : 32 * q + 4, :].bitcast(I32),
                     in_=c_proj_V_scales[0, 4 * q : 4 * q + 4, :].bitcast(I32))
-            load(1)
-            nc.sync.dma_start(out=bias_all[:], in_=c_proj_bias.partition_broadcast(P))
             load(2)
+            nc.sync.dma_start(out=bias_all[:], in_=c_proj_bias.partition_broadcast(P))
 
             cast(0)
+            product(0)
             us_product(0)
-            us_product(1)
             us_turn(0)
-            us_turn(1)
-            us_quant(0)
             cast(1)
+            us_product(1)
+            us_turn(1)
+            for i in range(1, LP):
+                product(i)
+            us_quant(0)
             us_quant(1)
-            nc.gpsimd.tensor_copy(out=bias_f32[:], in_=bias_all[:])
-            cast(2)
-            for i in range(PAIRS):
-                if i % 2 == 1 and (i + 5) // 2 < GROUPS:
-                    load((i + 5) // 2)
-                transposes(i)
-                vprod(i)
-                if i + 3 < PAIRS:
-                    cast(i + 3)
-                if i == 0:
+            for s in range(PAIRS + LF + 1):
+                if s % 2 == 1 and (s + 5) // 2 < GROUPS:
+                    load((s + 5) // 2)
+                for what in PEORDER:
+                    if what == "t0" and ok(s):
+                        banks0[s] = turn(wide_tiles[s], "bank0")
+                    if what == "t1" and ok(s):
+                        banks1[s] = turn(prod_tiles[s], "bank1")
+                    if what == "m0" and ok(s - LM):
+                        mx(s - LM, 0)
+                    if what == "m1" and ok(s - LM):
+                        mx(s - LM, 1)
+                for what in SORDER:
+                    if what == "x0" and ok(s - LX):
+                        exit0(s - LX)
+                    if what == "x1" and ok(s - LX):
+                        exit1(s - LX)
+                    if what == "c" and ok(s + LC) and s + LC > 1:
+                        cast(s + LC)
+                for what in VORDER:
+                    if what == "p" and ok(s + LP):
+                        product(s + LP)
+                    if what == "w" and ok(s - LW):
+                        weave(s - LW)
+                    if what == "q" and ok(s - LQ):
+                        quant(s - LQ)
+                    if what == "f0" and ok(s - LF):
+                        finish(s - LF, 0)
+                    if what == "f1" and ok(s - LF):
+                        finish(s - LF, 1)
+                if s == P_AT:
                     p_product(0)
-                if i == 1:
+                if s == P_AT + 1:
                     p_quant(0)
                     p_product(1)
-                if i == 2:
+                if s == P_AT + 2:
                     p_quant(1)
-                if i >= LAG:
-                    mx(i - LAG)
-                    finish(i - LAG)
-                    add_bias(i - LAG)
-                if i >= 1:
-                    quant(i - 1)
-            quant(PAIRS - 1)
-            for i in range(PAIRS - LAG, PAIRS):
-                mx(i)
-                finish(i)
-                add_bias(i)

@@ -20,12 +20,15 @@ COPY = mybir.ActivationFunctionType.Copy
 P = 128
 GROUPS = B * S // (4 * P)
 PAIRS = 2 * GROUPS
-LM, LX, LW, LQ, LF, LC, LP = 5, 0, 1, 1, 5, 2, 1
-VORDER = ("p", "w", "f0", "f1", "q")
-SORDER = ("x0", "x1", "c")
+LM, LX, LW, LQ, LF, LC, LP = 4, 0, 1, 2, 4, 2, 1
+VORDER = ("q", "w", "k", "f0", "p", "x", "f1")
+SORDER = ("x0", "c", "x1")
 PEORDER = ("t0", "m0", "t1", "m1")
-P_ON_V = 2
-P_AT = 2
+G_COLS = 512
+P_ON_V = 0
+P_AT = 1
+NB = 3
+SX = 32
 
 
 def tile_hybridsuperlayer_pb_t_w8_kernel(
@@ -57,7 +60,7 @@ def tile_hybridsuperlayer_pb_t_w8_kernel(
         p_grouped = const.tile([P, 2, D, 4], BF16, name="p_grouped", align_bytes=64)
         p_codes = const.tile([P, 2, D], U32, name="p_codes", align_bytes=64)
         p_scales = const.tile([P, 2, D], U8, name="p_scales", align_bytes=64)
-        scale_col = const.tile([P, 4], F32, name="scale_col")
+        scale_col = const.tile([P, 2, 4], F32, name="scale_col")
         scale_row = const.tile([P, 512], F32, name="scale_row")
         bias_all = const.tile([P, D], BF16, name="bias_all")
 
@@ -78,26 +81,32 @@ def tile_hybridsuperlayer_pb_t_w8_kernel(
             byte_tiles[n] = raw
 
         def cast(i):
-            wide = stage.tile([P, 2, 512], BF16, name="wide", tag="wide", bufs=LC + 2)
-            for a in range(2):
-                nc.scalar.copy(out=wide[:, a, :], in_=byte_tiles[i // 2][:, 2 * (i % 2) + a, 0:512].bitcast(E4M3))
+            j = 2 * (i % 2)
+            wide = stage.tile([P, 2, DFF], BF16, name="wide", tag="wide", bufs=LC + 2)
+            nc.scalar.copy(out=wide[:], in_=byte_tiles[i // 2][:, j : j + 2, :].bitcast(E4M3))
             wide_tiles[i] = wide
 
         def product(i):
-            prod = stage.tile([P, 2, 512], BF16, name="prod", tag="prod", bufs=LP + 2)
-            for a in range(2):
-                nc.vector.tensor_tensor(
-                    out=prod[:, a, :], in0=byte_tiles[i // 2][:, 2 * (i % 2) + a, 512:1024].bitcast(E4M3),
-                    in1=scale_row[:], op=MULT)
+            prod = stage.tile([P, 512], BF16, name="prod", tag="prod", bufs=LP + 2)
+            for c in range(0, 512, G_COLS):
+                nc.gpsimd.tensor_tensor(
+                    out=prod[:, c : c + G_COLS], in0=wide_tiles[i][:, 0, 512 + c : 512 + c + G_COLS],
+                    in1=scale_row[:, c : c + G_COLS], op=MULT)
             prod_tiles[i] = prod
 
         def turn(rows, tag):
             bank = psum.tile([P, 2, 2, P], F32, name=tag, tag=tag, bufs=2)
             for a in range(2):
-                words = rows[:, a, :].bitcast(F32)
+                words = rows[a].bitcast(F32)
                 for u in range(2):
                     nc.tensor.transpose(bank[:, u, a, :], words[:, u:256:2], ident[:])
             return bank
+
+        def grouped_of(i):
+            if i not in grouped_tiles:
+                grouped = stage.tile([P, 2, 2 * P, 4], BF16, name="grouped", tag="grouped", bufs=5, align_bytes=64)
+                grouped_tiles[i] = grouped
+            return grouped_tiles[i]
 
         def exit0(i):
             pair = stage.tile([P, 2, 2 * P, 2], BF16, name="pair", tag="pair", bufs=4)
@@ -106,19 +115,31 @@ def tile_hybridsuperlayer_pb_t_w8_kernel(
                 for e in range(2):
                     nc.scalar.activation(
                         out=pair[:, u, :, e], in_=halves[:, :, e], func=COPY,
-                        scale=scale_col[:, 2 * u + e : 2 * u + e + 1])
+                        scale=scale_col[:, 0, 2 * u + e : 2 * u + e + 1])
             pair_tiles[i] = pair
 
-        def exit1(i):
-            grouped = stage.tile([P, 2, 2 * P, 4], BF16, name="grouped", tag="grouped", bufs=5, align_bytes=64)
-            grouped_tiles[i] = grouped
-            nc.scalar.copy(
-                out=grouped[:, 1, :, :].rearrange("p x t -> p (x t)").bitcast(F32).rearrange("p (x u) -> p x u", u=2),
-                in_=banks1[i][:].rearrange("p u a r -> p (a r) u"))
+        def exit1(i, copy):
+            copy(
+                out=grouped_of(i)[:, 1, 0:P, :].rearrange("p x t -> p (x t)").bitcast(F32).rearrange("p (x u) -> p x u", u=2),
+                in_=banks1[i][:, :, 0, :].rearrange("p u r -> p r u"))
+
+        def product0(i):
+            nc.vector.tensor_tensor(
+                out=grouped_of(i)[:, 0, :, :].rearrange("p x (u e) -> p x u e", u=2),
+                in0=banks0[i][:].rearrange("p u a r -> p u (a r)").bitcast(BF16).rearrange("p u (x e) -> p x u e", e=2),
+                in1=scale_col[:, 0, :].rearrange("p (u e) -> p u e", u=2).unsqueeze(1).broadcast_to([P, 2 * P, 2, 2]),
+                op=MULT)
+
+        def scaled_exit1(i):
+            nc.vector.tensor_tensor(
+                out=grouped_of(i)[:, 1, P : 2 * P, :].rearrange("p x (u e) -> p x u e", u=2),
+                in0=banks1[i][:, :, 1, :].bitcast(BF16).rearrange("p u (x e) -> p x u e", e=2),
+                in1=scale_col[:, 1, :].rearrange("p (u e) -> p u e", u=2).unsqueeze(1).broadcast_to([P, P, 2, 2]),
+                op=MULT)
 
         def weave(i):
             nc.vector.tensor_copy(
-                out=grouped_tiles[i][:, 0, :, :].rearrange("p x t -> p (x t)").bitcast(F32).rearrange("p (x u) -> p x u", u=2),
+                out=grouped_of(i)[:, 0, :, :].rearrange("p x t -> p (x t)").bitcast(F32).rearrange("p (x u) -> p x u", u=2),
                 in_=pair_tiles[i][:].rearrange("p u x e -> p (u x e)").bitcast(F32).rearrange("p (u x) -> p x u", u=2))
 
         def quant(i):
@@ -192,11 +213,14 @@ def tile_hybridsuperlayer_pb_t_w8_kernel(
             return 0 <= i < PAIRS
 
         with tc.manual_schedule():
-            load(0)
-            nc.sync.dma_start(out=scale_row[:], in_=h_scale.rearrange("a o k -> (a o k)")[512:1024].partition_broadcast(P))
-            nc.sync.dma_start(out=s_all[:], in_=c_proj_S.partition_broadcast(P))
+            raw0 = stage.tile([P, 4, DFF], U8, name="raw", tag="raw", bufs=4)
+            byte_tiles[0] = raw0
+            nc.sync.dma_start(out=raw0[:, 0:2, :], in_=h_rows[0][:, 0:2, :])
+            nc.sync.dma_start(out=scale_col[:], in_=h_scale.rearrange("a o (g p t) -> p (a o g) t", g=2, t=4))
             nc.sync.dma_start(out=u_sb[:, 0], in_=u_rows[0])
-            nc.sync.dma_start(out=scale_col[:], in_=h_scale.rearrange("a o k -> (a o k)")[0:512].rearrange("(p t) -> p t", t=4))
+            nc.sync.dma_start(out=s_all[:], in_=c_proj_S.partition_broadcast(P))
+            nc.sync.dma_start(out=scale_row[:], in_=h_scale.rearrange("a o k -> (a o k)")[512:1024].partition_broadcast(P))
+            nc.sync.dma_start(out=raw0[:, 2:4, :], in_=h_rows[0][:, 2:4, :])
             nc.sync.dma_start(out=u_sb[:, 1], in_=u_rows[1])
             load(1)
             nc.sync.dma_start(out=v_words[:].bitcast(I32), in_=c_proj_V_words[0].rearrange("p n t -> p (n t)").bitcast(I32))
@@ -208,39 +232,51 @@ def tile_hybridsuperlayer_pb_t_w8_kernel(
             nc.sync.dma_start(out=bias_all[:], in_=c_proj_bias.partition_broadcast(P))
 
             cast(0)
-            product(0)
+            banks0[0] = turn((wide_tiles[0][:, 0, 0:512], wide_tiles[0][:, 1, 0:512]), "bank0")
             us_product(0)
-            us_turn(0)
             cast(1)
+            us_turn(0)
+            product(0)
+            product0(0)
+            banks1[0] = turn((prod_tiles[0][:], wide_tiles[0][:, 1, 512:1024]), "bank1")
             us_product(1)
             us_turn(1)
-            for i in range(1, LP):
-                product(i)
+            scaled_exit1(0)
+            exit1(0, nc.vector.tensor_copy)
             us_quant(0)
+            product(1)
+            cast(2)
             us_quant(1)
-            for s in range(PAIRS + LF + 1):
+            for s in range(1, PAIRS + LF + 1):
                 if s % 2 == 1 and (s + 5) // 2 < GROUPS:
                     load((s + 5) // 2)
                 for what in PEORDER:
                     if what == "t0" and ok(s):
-                        banks0[s] = turn(wide_tiles[s], "bank0")
+                        banks0[s] = turn((wide_tiles[s][:, 0, 0:512], wide_tiles[s][:, 1, 0:512]), "bank0")
                     if what == "t1" and ok(s):
-                        banks1[s] = turn(prod_tiles[s], "bank1")
+                        banks1[s] = turn((prod_tiles[s][:], wide_tiles[s][:, 1, 512:1024]), "bank1")
                     if what == "m0" and ok(s - LM):
                         mx(s - LM, 0)
                     if what == "m1" and ok(s - LM):
                         mx(s - LM, 1)
                 for what in SORDER:
-                    if what == "x0" and ok(s - LX):
+                    if what == "x0" and ok(s - LX) and s - LX >= NB:
                         exit0(s - LX)
-                    if what == "x1" and ok(s - LX):
-                        exit1(s - LX)
-                    if what == "c" and ok(s + LC) and s + LC > 1:
+                    if what == "x1" and ok(s) and s >= SX:
+                        exit1(s, nc.scalar.copy)
+                    if what == "c" and ok(s + LC) and s + LC > 2:
                         cast(s + LC)
                 for what in VORDER:
-                    if what == "p" and ok(s + LP):
-                        product(s + LP)
-                    if what == "w" and ok(s - LW):
+                    if what == "p" and ok(s):
+                        scaled_exit1(s)
+                    if what == "x" and ok(s) and s < SX:
+                        exit1(s, nc.vector.tensor_copy)
+                    if what == "k":
+                        if ok(s + LP) and s + LP > 1:
+                            product(s + LP)
+                    if what == "w" and ok(s) and s < NB:
+                        product0(s)
+                    if what == "w" and ok(s - LW) and s - LW >= NB:
                         weave(s - LW)
                     if what == "q" and ok(s - LQ):
                         quant(s - LQ)

@@ -3,8 +3,8 @@ from contextlib import ExitStack
 import concourse.mybir as mybir
 from concourse.masks import make_identity
 
-B, S, D, DFF, R = 4, 2048, 512, 1024, 512
-FLOPS = 2 * B * S * DFF * D + 2 * DFF * R * D
+BATCH, SEQ, OUT, HIDDEN, RANK = 4, 2048, 512, 1024, 512
+FLOPS = 2 * BATCH * SEQ * HIDDEN * OUT + 2 * HIDDEN * RANK * OUT
 
 F32 = mybir.dt.float32
 BF16 = mybir.dt.bfloat16
@@ -12,282 +12,348 @@ U32 = mybir.dt.uint32
 I32 = mybir.dt.int32
 U8 = mybir.dt.uint8
 E4M3 = mybir.dt.float8_e4m3fn
-X4 = mybir.dt.float8_e4m3fn_x4
+E4M3_X4 = mybir.dt.float8_e4m3fn_x4
 MULT = mybir.AluOpType.mult
 ADD = mybir.AluOpType.add
 COPY = mybir.ActivationFunctionType.Copy
 
-P = 128
-GROUPS = B * S // (4 * P)
-PAIRS = 2 * GROUPS
-LM, LX, LW, LQ, LF, LC, LP = 4, 0, 1, 2, 4, 2, 1
-VORDER = ("q", "w", "k", "f0", "p", "x", "f1")
-SORDER = ("x0", "c", "x1")
-PEORDER = ("t0", "m0", "t1", "m1")
-G_COLS = 512
-P_ON_V = 0
-P_AT = 1
-NB = 3
-SX = 32
+PART = 128
+K_PASS = 512
+QUADS = BATCH * SEQ // (4 * PART)
+PAIRS = 2 * QUADS
+
+WIDEN_AHEAD = 3
+WEAVE_BEHIND = 2
+QUANTISE_BEHIND = 3
+MULTIPLY_BEHIND = 5
+
+FIRST_BY_SCALAR = 4
+FIRST_EMPTIED_BY_SCALAR = PAIRS - 4
 
 
 def tile_hybridsuperlayer_pb_t_w8_kernel(
     tc, h_bytes, h_scale, c_proj_U, c_proj_S, c_proj_V_words, c_proj_V_scales, c_proj_bias, out
 ):
     nc = tc.nc
-    h_rows = h_bytes.rearrange("b s k -> (b s) k").rearrange("(n p j) k -> n p j k", p=P, j=4)
-    out_rows = out.rearrange("b s d -> (b s) d").rearrange("(n p j) d -> n p j d", p=P, j=4)
+    h_rows = h_bytes.rearrange("b s k -> (b s) k").rearrange("(n p j) k -> n p j k", p=PART, j=4)
+    out_rows = out.rearrange("b s d -> (b s) d").rearrange("(n p j) d -> n p j d", p=PART, j=4)
     u_rows = c_proj_U.rearrange("(g m t) r -> g m t r", g=2, t=4)
 
     with ExitStack() as ctx:
-        const = ctx.enter_context(tc.tile_pool(name="const", bufs=1))
+        keep = ctx.enter_context(tc.tile_pool(name="keep", bufs=1))
         stage = ctx.enter_context(tc.tile_pool(name="stage", bufs=3))
-        codes_pool = ctx.enter_context(tc.tile_pool(name="codes", bufs=LM + 3))
-        psum = ctx.enter_context(tc.psum_pool(name="psum", bufs=2))
+        quantised = ctx.enter_context(tc.tile_pool(name="quantised", bufs=MULTIPLY_BEHIND + 3))
+        psum = ctx.enter_context(tc.psum_pool(name="psum", bufs=3))
 
-        ident = const.tile([P, P], F32, name="ident")
+        ident = keep.tile([PART, PART], F32, name="ident")
         make_identity(nc, ident[:])
-        v_scales = const.tile([P, D], U8, name="v_scales", align_bytes=64)
+        v_scales = keep.tile([PART, OUT], U8, name="v_scales", align_bytes=64)
         nc.gpsimd.memset(v_scales[:].bitcast(I32), 0)
 
-        s_all = const.tile([P, R], BF16, name="s_all")
-        u_sb = const.tile([P, 2, 4, R], BF16, name="u_sb")
-        us = const.tile([P, 2, 4, R], BF16, name="us")
-        us_grouped = const.tile([P, 2, 4, P, 4], BF16, name="us_grouped", align_bytes=64)
-        us_codes = const.tile([P, 2, 4 * P], U32, name="us_codes", align_bytes=64)
-        us_scales = const.tile([P, 2, 4 * P], U8, name="us_scales", align_bytes=64)
-        v_words = const.tile([P, 4 * D], U8, name="v_words", align_bytes=64)
-        p_grouped = const.tile([P, 2, D, 4], BF16, name="p_grouped", align_bytes=64)
-        p_codes = const.tile([P, 2, D], U32, name="p_codes", align_bytes=64)
-        p_scales = const.tile([P, 2, D], U8, name="p_scales", align_bytes=64)
-        scale_col = const.tile([P, 2, 4], F32, name="scale_col")
-        scale_row = const.tile([P, 512], F32, name="scale_row")
-        bias_all = const.tile([P, D], BF16, name="bias_all")
+        s_col = keep.tile([PART, 4], BF16, name="s_col")
+        u_raw = keep.tile([PART, 2, 4, RANK], BF16, name="u_raw")
+        us_grouped = keep.tile([PART, 2, 4, PART, 4], BF16, name="us_grouped", align_bytes=64)
+        us_codes = keep.tile([PART, 2, 4 * PART], U32, name="us_codes", align_bytes=64)
+        us_scales = keep.tile([PART, 2, 4 * PART], U8, name="us_scales", align_bytes=64)
+        v_words = keep.tile([PART, 4 * OUT], U8, name="v_words", align_bytes=64)
+        p_grouped = keep.tile([PART, 2, OUT, 4], BF16, name="p_grouped", align_bytes=64)
+        p_codes = keep.tile([PART, 2, OUT], U32, name="p_codes", align_bytes=64)
+        p_scales = keep.tile([PART, 2, OUT], U8, name="p_scales", align_bytes=64)
+        scale_col = keep.tile([PART, 2, 4], F32, name="scale_col")
+        scale_row = keep.tile([PART, K_PASS], F32, name="scale_row")
+        bias_col = keep.tile([PART, 4], BF16, name="bias_col")
+        bias_col_f32 = keep.tile([PART, 4], F32, name="bias_col_f32")
+        bias_row = keep.tile([PART, OUT], F32, name="bias_row")
 
         byte_tiles = {}
         wide_tiles = {}
-        prod_tiles = {}
-        banks0 = {}
-        banks1 = {}
-        pair_tiles = {}
+        product_tiles = {}
+        low_banks = {}
+        high_banks = {}
+        half_tiles = {}
         grouped_tiles = {}
         code_tiles = {}
-        out_banks = {}
-        res_tiles = {}
+        sum_banks = {}
+        result_tiles = {}
+
+
+        def spread(row, col):
+            bank = psum.tile([PART, 4, PART], F32, name="sums", tag="sums")
+            for t in range(4):
+                nc.tensor.transpose(bank[:, t, :], col[:, t : t + 1].to_broadcast([PART, PART]), ident[:])
+            nc.scalar.copy(out=row[:].rearrange("p (n t) -> p n t", t=4), in_=bank[:].rearrange("p t n -> p n t"))
+
+        def turn(bank, rows, u):
+            nc.tensor.transpose(bank, rows.bitcast(F32)[:, u : K_PASS // 2 : 2], ident[:])
+
+        def scale_out(grouped, bank, factors):
+            columns = grouped.shape[1]
+            nc.vector.tensor_tensor(
+                out=grouped.rearrange("p x (u e) -> p x u e", u=2),
+                in0=bank.bitcast(BF16).rearrange("p u (x e) -> p x u e", e=2),
+                in1=factors.rearrange("p (u e) -> p u e", u=2).unsqueeze(1).broadcast_to([PART, columns, 2, 2]),
+                op=MULT,
+            )
+
+        def as_words(grouped):
+            return grouped.rearrange("p x t -> p (x t)").bitcast(F32).rearrange("p (x u) -> p x u", u=2)
+
+
+        def turn_u(g):
+            for t0 in (0, 2):
+                bank = psum.tile([PART, 2, 2, PART], F32, name="sums", tag="sums")
+                for a in range(2):
+                    for u in range(2):
+                        turn(bank[:, u, a, :], u_raw[:, g, t0 + a, :], u)
+                scale_out(
+                    us_grouped[:, g, t0 : t0 + 2, :, :].rearrange("p a m x -> p (a m) x"),
+                    bank[:].rearrange("p u a m -> p u (a m)"),
+                    s_col[:],
+                )
+
+        def quantise_us(g):
+            nc.vector.quantize_mx(
+                out=us_codes[:, g, :].bitcast(E4M3_X4),
+                scales=us_scales[:, g, :],
+                in_=us_grouped[:, g].rearrange("p t m x -> p (t m x)"),
+            )
+
+        def multiply_us(g):
+            for c in range(4):
+                bank = psum.tile([PART, 4, PART], F32, name="sums", tag="sums")
+                for t in range(4):
+                    nc.tensor.matmul_mx(
+                        out=bank[:, t, :],
+                        lhsT=us_codes[:, g, t * PART : (t + 1) * PART].bitcast(E4M3_X4),
+                        lhsT_scale=us_scales[:, g, t * PART : (t + 1) * PART],
+                        rhs=v_words[:, 4 * PART * c : 4 * PART * (c + 1)].bitcast(E4M3_X4),
+                        rhs_scale=v_scales[:, PART * c : PART * (c + 1)],
+                        start=True,
+                        stop=True,
+                    )
+                nc.scalar.copy(
+                    out=p_grouped[:, g, PART * c : PART * (c + 1), :], in_=bank[:].rearrange("p t n -> p n t")
+                )
+
+        def quantise_p(g):
+            nc.vector.quantize_mx(
+                out=p_codes[:, g, :].bitcast(E4M3_X4),
+                scales=p_scales[:, g, :],
+                in_=p_grouped[:, g].rearrange("p n t -> p (n t)"),
+            )
+
 
         def load(n):
-            raw = stage.tile([P, 4, DFF], U8, name="raw", tag="raw", bufs=4)
+            raw = stage.tile([PART, 4, HIDDEN], U8, name="raw", tag="raw", bufs=4)
             nc.sync.dma_start(out=raw[:], in_=h_rows[n])
             byte_tiles[n] = raw
 
-        def cast(i):
+        def widen(i):
             j = 2 * (i % 2)
-            wide = stage.tile([P, 2, DFF], BF16, name="wide", tag="wide", bufs=LC + 2)
+            wide = stage.tile([PART, 2, HIDDEN], BF16, name="wide", tag="wide", bufs=WIDEN_AHEAD + 2)
             nc.scalar.copy(out=wide[:], in_=byte_tiles[i // 2][:, j : j + 2, :].bitcast(E4M3))
             wide_tiles[i] = wide
 
-        def product(i):
-            prod = stage.tile([P, 512], BF16, name="prod", tag="prod", bufs=LP + 2)
-            for c in range(0, 512, G_COLS):
-                nc.gpsimd.tensor_tensor(
-                    out=prod[:, c : c + G_COLS], in0=wide_tiles[i][:, 0, 512 + c : 512 + c + G_COLS],
-                    in1=scale_row[:, c : c + G_COLS], op=MULT)
-            prod_tiles[i] = prod
+        def scale_tile0(i):
+            product = stage.tile([PART, K_PASS], BF16, name="product", tag="product")
+            nc.gpsimd.tensor_tensor(out=product[:], in0=wide_tiles[i][:, 0, K_PASS:], in1=scale_row[:], op=MULT)
+            product_tiles[i] = product
 
-        def turn(rows, tag):
-            bank = psum.tile([P, 2, 2, P], F32, name=tag, tag=tag, bufs=2)
-            for a in range(2):
-                words = rows[a].bitcast(F32)
+        def turn_low(i):
+            if i < FIRST_BY_SCALAR:
+                bank = psum.tile([PART, 2, 2, PART], F32, name="low", tag="low", bufs=2)
+                for a in range(2):
+                    for u in range(2):
+                        turn(bank[:, u, a, :], wide_tiles[i][:, a, 0:K_PASS], u)
+            else:
+                u = i % 2
+                bank = psum.tile([PART, 4, PART], F32, name="low", tag="low", bufs=2)
+                for j in range(4):
+                    turn(bank[:, j, :], wide_tiles[i - u + j // 2][:, j % 2, 0:K_PASS], u)
+            low_banks[i] = bank
+
+        def turn_high(i):
+            for a, rows in ((1, wide_tiles[i][:, 1, K_PASS:]), (0, product_tiles[i][:])):
+                bank = psum.tile([PART, 2, PART], F32, name="high", tag="high")
                 for u in range(2):
-                    nc.tensor.transpose(bank[:, u, a, :], words[:, u:256:2], ident[:])
-            return bank
+                    turn(bank[:, u, :], rows, u)
+                high_banks[i, a] = bank
 
         def grouped_of(i):
             if i not in grouped_tiles:
-                grouped = stage.tile([P, 2, 2 * P, 4], BF16, name="grouped", tag="grouped", bufs=5, align_bytes=64)
+                grouped = stage.tile(
+                    [PART, 2, 2 * PART, 4], BF16, name="grouped", tag="grouped", bufs=6, align_bytes=64
+                )
                 grouped_tiles[i] = grouped
             return grouped_tiles[i]
 
-        def exit0(i):
-            pair = stage.tile([P, 2, 2 * P, 2], BF16, name="pair", tag="pair", bufs=4)
-            for u in range(2):
-                halves = banks0[i][:, u, :, :].rearrange("p a r -> p (a r)").bitcast(BF16).rearrange("p (x e) -> p x e", e=2)
-                for e in range(2):
-                    nc.scalar.activation(
-                        out=pair[:, u, :, e], in_=halves[:, :, e], func=COPY,
-                        scale=scale_col[:, 0, 2 * u + e : 2 * u + e + 1])
-            pair_tiles[i] = pair
+        def scale_low_by_vector(i):
+            scale_out(
+                grouped_of(i)[:, 0, :, :], low_banks[i][:].rearrange("p u a r -> p u (a r)"), scale_col[:, 0, :]
+            )
 
-        def exit1(i, copy):
-            copy(
-                out=grouped_of(i)[:, 1, 0:P, :].rearrange("p x t -> p (x t)").bitcast(F32).rearrange("p (x u) -> p x u", u=2),
-                in_=banks1[i][:, :, 0, :].rearrange("p u r -> p r u"))
-
-        def product0(i):
-            nc.vector.tensor_tensor(
-                out=grouped_of(i)[:, 0, :, :].rearrange("p x (u e) -> p x u e", u=2),
-                in0=banks0[i][:].rearrange("p u a r -> p u (a r)").bitcast(BF16).rearrange("p u (x e) -> p x u e", e=2),
-                in1=scale_col[:, 0, :].rearrange("p (u e) -> p u e", u=2).unsqueeze(1).broadcast_to([P, 2 * P, 2, 2]),
-                op=MULT)
-
-        def scaled_exit1(i):
-            nc.vector.tensor_tensor(
-                out=grouped_of(i)[:, 1, P : 2 * P, :].rearrange("p x (u e) -> p x u e", u=2),
-                in0=banks1[i][:, :, 1, :].bitcast(BF16).rearrange("p u (x e) -> p x u e", e=2),
-                in1=scale_col[:, 1, :].rearrange("p (u e) -> p u e", u=2).unsqueeze(1).broadcast_to([P, P, 2, 2]),
-                op=MULT)
+        def scale_low_by_scalar(i):
+            u = i % 2
+            if u == 0:
+                halves = stage.tile([PART, 2, 4 * PART, 2], BF16, name="halves", tag="halves")
+                half_tiles[i // 2] = halves
+            words = low_banks[i][:].rearrange("p j r -> p (j r)").bitcast(BF16).rearrange("p (x e) -> p x e", e=2)
+            for e in range(2):
+                nc.scalar.activation(
+                    out=half_tiles[i // 2][:, u, :, e],
+                    in_=words[:, :, e],
+                    func=COPY,
+                    scale=scale_col[:, 0, 2 * u + e : 2 * u + e + 1],
+                )
 
         def weave(i):
+            words = half_tiles[i // 2][:].rearrange("p u x e -> p (u x e)").bitcast(F32)
+            columns = slice(2 * PART * (i % 2), 2 * PART * (i % 2 + 1))
             nc.vector.tensor_copy(
-                out=grouped_of(i)[:, 0, :, :].rearrange("p x t -> p (x t)").bitcast(F32).rearrange("p (x u) -> p x u", u=2),
-                in_=pair_tiles[i][:].rearrange("p u x e -> p (u x e)").bitcast(F32).rearrange("p (u x) -> p x u", u=2))
+                out=as_words(grouped_of(i)[:, 0, :, :]),
+                in_=words.rearrange("p (u x) -> p x u", u=2)[:, columns, :],
+            )
 
-        def quant(i):
-            codes = codes_pool.tile([P, 2, 2 * P], U32, name="codes", align_bytes=64)
-            scales = codes_pool.tile([P, 2, 2 * P], U8, name="scales", align_bytes=64)
+        def empty_high0(i, copy):
+            copy(
+                out=as_words(grouped_of(i)[:, 1, 0:PART, :]), in_=high_banks[i, 0][:].rearrange("p u r -> p r u")
+            )
+
+        def scale_high1(i):
+            scale_out(grouped_of(i)[:, 1, PART:, :], high_banks[i, 1][:], scale_col[:, 1, :])
+
+        def quantise(i):
+            codes = quantised.tile([PART, 2, 2 * PART], U32, name="codes", align_bytes=64)
+            scales = quantised.tile([PART, 2, 2 * PART], U8, name="scales", align_bytes=64)
             nc.vector.quantize_mx(
-                out=codes[:].rearrange("p g x -> p (g x)").bitcast(X4),
+                out=codes[:].rearrange("p g x -> p (g x)").bitcast(E4M3_X4),
                 scales=scales[:].rearrange("p g x -> p (g x)"),
-                in_=grouped_tiles[i][:].rearrange("p g x t -> p (g x t)"))
+                in_=grouped_tiles[i][:].rearrange("p g x t -> p (g x t)"),
+            )
             code_tiles[i] = (codes, scales)
 
-        def mx(i, a):
+        def multiply(i, a):
             codes, scales = code_tiles[i]
-            bank = psum.tile([P, D], F32, name="acc", tag="acc", bufs=4)
+            tokens = slice(PART * a, PART * (a + 1))
+            bank = psum.tile([PART, OUT], F32, name="sums", tag="sums")
             for g in range(2):
                 nc.tensor.matmul_mx(
-                    out=bank[:], lhsT=codes[:, g, P * a : P * (a + 1)].bitcast(X4), lhsT_scale=scales[:, g, P * a : P * (a + 1)],
-                    rhs=p_codes[:, g, :].bitcast(X4), rhs_scale=p_scales[:, g, :],
-                    start=(g == 0), stop=(g == 1))
-            out_banks[i, a] = bank
+                    out=bank[:],
+                    lhsT=codes[:, g, tokens].bitcast(E4M3_X4),
+                    lhsT_scale=scales[:, g, tokens],
+                    rhs=p_codes[:, g, :].bitcast(E4M3_X4),
+                    rhs_scale=p_scales[:, g, :],
+                    start=(g == 0),
+                    stop=(g == 1),
+                )
+            sum_banks[i, a] = bank
 
         def finish(i, a):
             if a == 0:
-                res = stage.tile([P, 2, D], F32, name="res", tag="res", bufs=4)
-                res_tiles[i] = res
-            nc.vector.tensor_tensor(out=res_tiles[i][:, a, :], in0=out_banks[i, a][:], in1=bias_all[:], op=ADD)
-            if i == PAIRS - 1:
-                j = 2 * (i % 2) + a
-                nc.sync.dma_start(out=out_rows[i // 2][:, j, :], in_=res_tiles[i][:, a, :])
+                result = stage.tile([PART, 2, OUT], F32, name="result", tag="result", bufs=5)
+                result_tiles[i] = result
+            result = result_tiles[i]
+            nc.vector.tensor_tensor(out=result[:, a, :], in0=sum_banks[i, a][:], in1=bias_row[:], op=ADD)
+            j = 2 * (i % 2)
+            if i >= PAIRS - MULTIPLY_BEHIND:
+                nc.sync.dma_start(out=out_rows[i // 2][:, j + a, :], in_=result[:, a, :])
             elif a == 1:
-                j = 2 * (i % 2)
-                nc.sync.dma_start(out=out_rows[i // 2][:, j : j + 2, :], in_=res_tiles[i][:])
-
-        def us_product(g):
-            nc.vector.tensor_tensor(out=us[:, g], in0=u_sb[:, g], in1=s_all[:].unsqueeze(1).broadcast_to([P, 4, R]), op=MULT)
-
-        def us_turn(g):
-            for t0 in (0, 2):
-                bank = psum.tile([P, 2, 2, P], F32, name="acc", tag="acc", bufs=4)
-                for a in range(2):
-                    words = us[:, g, t0 + a, :].bitcast(F32)
-                    for u in range(2):
-                        nc.tensor.transpose(bank[:, a, u, :], words[:, u : 256 : 2], ident[:])
-                nc.scalar.copy(
-                    out=us_grouped[:, g, t0 : t0 + 2, :, :].rearrange("p a m t -> p (a m t)").bitcast(F32).rearrange("p (a m u) -> p a m u", a=2, u=2),
-                    in_=bank[:].rearrange("p a u m -> p a m u"))
-
-        def us_quant(g):
-            nc.vector.quantize_mx(
-                out=us_codes[:, g, :].bitcast(X4), scales=us_scales[:, g, :],
-                in_=us_grouped[:, g].rearrange("p t m x -> p (t m x)"))
-
-        def p_product(g):
-            for c in range(4):
-                bank = psum.tile([P, 4, P], F32, name="acc", tag="acc", bufs=4)
-                for t in range(4):
-                    nc.tensor.matmul_mx(
-                        out=bank[:, t, :], lhsT=us_codes[:, g, t * P : (t + 1) * P].bitcast(X4),
-                        lhsT_scale=us_scales[:, g, t * P : (t + 1) * P],
-                        rhs=v_words[:, 4 * P * c : 4 * P * (c + 1)].bitcast(X4),
-                        rhs_scale=v_scales[:, P * c : P * (c + 1)], start=True, stop=True)
-                copy = nc.vector.tensor_copy if c < P_ON_V else nc.scalar.copy
-                copy(out=p_grouped[:, g, P * c : P * (c + 1), :], in_=bank[:].rearrange("p t n -> p n t"))
-
-        def p_quant(g):
-            nc.vector.quantize_mx(
-                out=p_codes[:, g, :].bitcast(X4), scales=p_scales[:, g, :],
-                in_=p_grouped[:, g].rearrange("p n t -> p (n t)"))
-
-        def ok(i):
-            return 0 <= i < PAIRS
+                nc.sync.dma_start(out=out_rows[i // 2][:, j : j + 2, :], in_=result[:])
 
         with tc.manual_schedule():
-            raw0 = stage.tile([P, 4, DFF], U8, name="raw", tag="raw", bufs=4)
+            nc.sync.dma_start(out=s_col[:], in_=c_proj_S.rearrange("(p t) -> p t", t=4))
+            nc.sync.dma_start(out=scale_col[:], in_=h_scale.rearrange("a o (g p t) -> p (a o g) t", g=2, t=4))
+            raw0 = stage.tile([PART, 4, HIDDEN], U8, name="raw", tag="raw", bufs=4)
             byte_tiles[0] = raw0
             nc.sync.dma_start(out=raw0[:, 0:2, :], in_=h_rows[0][:, 0:2, :])
-            nc.sync.dma_start(out=scale_col[:], in_=h_scale.rearrange("a o (g p t) -> p (a o g) t", g=2, t=4))
-            nc.sync.dma_start(out=u_sb[:, 0], in_=u_rows[0])
-            nc.sync.dma_start(out=s_all[:], in_=c_proj_S.partition_broadcast(P))
-            nc.sync.dma_start(out=scale_row[:], in_=h_scale.rearrange("a o k -> (a o k)")[512:1024].partition_broadcast(P))
+            nc.sync.dma_start(out=u_raw[:, 0], in_=u_rows[0])
             nc.sync.dma_start(out=raw0[:, 2:4, :], in_=h_rows[0][:, 2:4, :])
-            nc.sync.dma_start(out=u_sb[:, 1], in_=u_rows[1])
+            nc.sync.dma_start(out=u_raw[:, 1], in_=u_rows[1])
             load(1)
-            nc.sync.dma_start(out=v_words[:].bitcast(I32), in_=c_proj_V_words[0].rearrange("p n t -> p (n t)").bitcast(I32))
+            nc.sync.dma_start(
+                out=v_words[:].bitcast(I32), in_=c_proj_V_words[0].rearrange("p n t -> p (n t)").bitcast(I32)
+            )
             for q in range(4):
                 nc.sync.dma_start(
                     out=v_scales[32 * q : 32 * q + 4, :].bitcast(I32),
-                    in_=c_proj_V_scales[0, 4 * q : 4 * q + 4, :].bitcast(I32))
+                    in_=c_proj_V_scales[0, 4 * q : 4 * q + 4, :].bitcast(I32),
+                )
             load(2)
-            nc.sync.dma_start(out=bias_all[:], in_=c_proj_bias.partition_broadcast(P))
+            nc.sync.dma_start(out=bias_col[:], in_=c_proj_bias.rearrange("(p t) -> p t", t=4))
 
-            cast(0)
-            banks0[0] = turn((wide_tiles[0][:, 0, 0:512], wide_tiles[0][:, 1, 0:512]), "bank0")
-            us_product(0)
-            cast(1)
-            us_turn(0)
-            product(0)
-            product0(0)
-            banks1[0] = turn((prod_tiles[0][:], wide_tiles[0][:, 1, 512:1024]), "bank1")
-            us_product(1)
-            us_turn(1)
-            scaled_exit1(0)
-            exit1(0, nc.vector.tensor_copy)
-            us_quant(0)
-            product(1)
-            cast(2)
-            us_quant(1)
-            for s in range(1, PAIRS + LF + 1):
-                if s % 2 == 1 and (s + 5) // 2 < GROUPS:
-                    load((s + 5) // 2)
-                for what in PEORDER:
-                    if what == "t0" and ok(s):
-                        banks0[s] = turn((wide_tiles[s][:, 0, 0:512], wide_tiles[s][:, 1, 0:512]), "bank0")
-                    if what == "t1" and ok(s):
-                        banks1[s] = turn((prod_tiles[s][:], wide_tiles[s][:, 1, 512:1024]), "bank1")
-                    if what == "m0" and ok(s - LM):
-                        mx(s - LM, 0)
-                    if what == "m1" and ok(s - LM):
-                        mx(s - LM, 1)
-                for what in SORDER:
-                    if what == "x0" and ok(s - LX) and s - LX >= NB:
-                        exit0(s - LX)
-                    if what == "x1" and ok(s) and s >= SX:
-                        exit1(s, nc.scalar.copy)
-                    if what == "c" and ok(s + LC) and s + LC > 2:
-                        cast(s + LC)
-                for what in VORDER:
-                    if what == "p" and ok(s):
-                        scaled_exit1(s)
-                    if what == "x" and ok(s) and s < SX:
-                        exit1(s, nc.vector.tensor_copy)
-                    if what == "k":
-                        if ok(s + LP) and s + LP > 1:
-                            product(s + LP)
-                    if what == "w" and ok(s) and s < NB:
-                        product0(s)
-                    if what == "w" and ok(s - LW) and s - LW >= NB:
-                        weave(s - LW)
-                    if what == "q" and ok(s - LQ):
-                        quant(s - LQ)
-                    if what == "f0" and ok(s - LF):
-                        finish(s - LF, 0)
-                    if what == "f1" and ok(s - LF):
-                        finish(s - LF, 1)
-                if s == P_AT:
-                    p_product(0)
-                if s == P_AT + 1:
-                    p_quant(0)
-                    p_product(1)
-                if s == P_AT + 2:
-                    p_quant(1)
+            spread(scale_row, scale_col[:, 1, :])
+            widen(0)
+            turn_u(0)
+            turn_low(0)
+            scale_tile0(0)
+            widen(1)
+            widen(2)
+            turn_high(0)
+            quantise_us(0)
+            widen(3)
+            turn_u(1)
+            scale_high1(0)
+            scale_low_by_vector(0)
+            empty_high0(0, nc.vector.tensor_copy)
+            scale_tile0(1)
+            multiply_us(0)
+            quantise_us(1)
+
+            for i in range(1, PAIRS):
+                done = i - MULTIPLY_BEHIND
+                if i % 2 == 1 and (i + 5) // 2 < QUADS:
+                    load((i + 5) // 2)
+
+                turn_low(i)
+                if done >= 0:
+                    multiply(done, 0)
+                turn_high(i)
+                if done >= 0:
+                    multiply(done, 1)
+
+                if i >= FIRST_BY_SCALAR:
+                    scale_low_by_scalar(i)
+                if i + WIDEN_AHEAD < PAIRS:
+                    widen(i + WIDEN_AHEAD)
+                if i >= FIRST_EMPTIED_BY_SCALAR:
+                    empty_high0(i, nc.scalar.copy)
+
+                if done >= 0:
+                    finish(done, 0)
+                scale_high1(i)
+                if i >= QUANTISE_BEHIND:
+                    quantise(i - QUANTISE_BEHIND)
+                if i < FIRST_BY_SCALAR:
+                    scale_low_by_vector(i)
+                if i - WEAVE_BEHIND >= FIRST_BY_SCALAR:
+                    weave(i - WEAVE_BEHIND)
+                if i < FIRST_EMPTIED_BY_SCALAR:
+                    empty_high0(i, nc.vector.tensor_copy)
+                if done >= 0:
+                    finish(done, 1)
+
+                if i + 1 < PAIRS:
+                    scale_tile0(i + 1)
+
+                if i == 2:
+                    nc.scalar.copy(out=bias_col_f32[:], in_=bias_col[:])
+                    spread(bias_row, bias_col_f32[:])
+                    quantise_p(0)
+                    multiply_us(1)
+                if i == 3:
+                    quantise_p(1)
+
+            last = PAIRS - 1
+            weave(last - 1)
+            quantise(last - 2)
+            for i in range(PAIRS - MULTIPLY_BEHIND, PAIRS):
+                if i == last - 3:
+                    weave(last)
+                if i == last - 2:
+                    quantise(last - 1)
+                if i == last - 1:
+                    quantise(last)
+                multiply(i, 0)
+                multiply(i, 1)
+                finish(i, 0)
+                finish(i, 1)

from contextlib import ExitStack

import concourse.mybir as mybir
from concourse.masks import make_identity

BATCH, SEQ, OUT, HIDDEN, RANK = 4, 2048, 512, 1024, 512
FLOPS = 2 * BATCH * SEQ * HIDDEN * OUT + 2 * HIDDEN * RANK * OUT

F32 = mybir.dt.float32
BF16 = mybir.dt.bfloat16
U32 = mybir.dt.uint32
I32 = mybir.dt.int32
U8 = mybir.dt.uint8
E4M3 = mybir.dt.float8_e4m3fn
E4M3_X4 = mybir.dt.float8_e4m3fn_x4
MULT = mybir.AluOpType.mult
ADD = mybir.AluOpType.add
COPY = mybir.ActivationFunctionType.Copy

PART = 128
K_PASS = 512
QUADS = BATCH * SEQ // (4 * PART)
PAIRS = 2 * QUADS

WIDEN_AHEAD = 3
WEAVE_BEHIND = 2
QUANTISE_BEHIND = 3
MULTIPLY_BEHIND = 5

FIRST_BY_SCALAR = 4
FIRST_EMPTIED_BY_SCALAR = PAIRS - 4


def tile_hybridsuperlayer_pb_t_w8_kernel(
    tc, h_bytes, h_scale, c_proj_U, c_proj_S, c_proj_V_words, c_proj_V_scales, c_proj_bias, out
):
    nc = tc.nc
    h_rows = h_bytes.rearrange("b s k -> (b s) k").rearrange("(n p j) k -> n p j k", p=PART, j=4)
    out_rows = out.rearrange("b s d -> (b s) d").rearrange("(n p j) d -> n p j d", p=PART, j=4)
    u_rows = c_proj_U.rearrange("(g m t) r -> g m t r", g=2, t=4)

    with ExitStack() as ctx:
        keep = ctx.enter_context(tc.tile_pool(name="keep", bufs=1))
        stage = ctx.enter_context(tc.tile_pool(name="stage", bufs=3))
        quantised = ctx.enter_context(tc.tile_pool(name="quantised", bufs=MULTIPLY_BEHIND + 3))
        psum = ctx.enter_context(tc.psum_pool(name="psum", bufs=3))

        ident = keep.tile([PART, PART], F32, name="ident")
        make_identity(nc, ident[:])
        v_scales = keep.tile([PART, OUT], U8, name="v_scales", align_bytes=64)
        nc.gpsimd.memset(v_scales[:].bitcast(I32), 0)

        s_col = keep.tile([PART, 4], BF16, name="s_col")
        u_raw = keep.tile([PART, 2, 4, RANK], BF16, name="u_raw")
        us_grouped = keep.tile([PART, 2, 4, PART, 4], BF16, name="us_grouped", align_bytes=64)
        us_codes = keep.tile([PART, 2, 4 * PART], U32, name="us_codes", align_bytes=64)
        us_scales = keep.tile([PART, 2, 4 * PART], U8, name="us_scales", align_bytes=64)
        v_words = keep.tile([PART, 4 * OUT], U8, name="v_words", align_bytes=64)
        p_grouped = keep.tile([PART, 2, OUT, 4], BF16, name="p_grouped", align_bytes=64)
        p_codes = keep.tile([PART, 2, OUT], U32, name="p_codes", align_bytes=64)
        p_scales = keep.tile([PART, 2, OUT], U8, name="p_scales", align_bytes=64)
        scale_col = keep.tile([PART, 2, 4], F32, name="scale_col")
        scale_row = keep.tile([PART, K_PASS], F32, name="scale_row")
        bias_col = keep.tile([PART, 4], BF16, name="bias_col")
        bias_col_f32 = keep.tile([PART, 4], F32, name="bias_col_f32")
        bias_row = keep.tile([PART, OUT], F32, name="bias_row")

        byte_tiles = {}
        wide_tiles = {}
        product_tiles = {}
        low_banks = {}
        high_banks = {}
        half_tiles = {}
        grouped_tiles = {}
        code_tiles = {}
        sum_banks = {}
        result_tiles = {}


        def spread(row, col):
            bank = psum.tile([PART, 4, PART], F32, name="sums", tag="sums")
            for t in range(4):
                nc.tensor.transpose(bank[:, t, :], col[:, t : t + 1].to_broadcast([PART, PART]), ident[:])
            nc.scalar.copy(out=row[:].rearrange("p (n t) -> p n t", t=4), in_=bank[:].rearrange("p t n -> p n t"))

        def turn(bank, rows, u):
            nc.tensor.transpose(bank, rows.bitcast(F32)[:, u : K_PASS // 2 : 2], ident[:])

        def scale_out(grouped, bank, factors):
            columns = grouped.shape[1]
            nc.vector.tensor_tensor(
                out=grouped.rearrange("p x (u e) -> p x u e", u=2),
                in0=bank.bitcast(BF16).rearrange("p u (x e) -> p x u e", e=2),
                in1=factors.rearrange("p (u e) -> p u e", u=2).unsqueeze(1).broadcast_to([PART, columns, 2, 2]),
                op=MULT,
            )

        def as_words(grouped):
            return grouped.rearrange("p x t -> p (x t)").bitcast(F32).rearrange("p (x u) -> p x u", u=2)


        def turn_u(g):
            for t0 in (0, 2):
                bank = psum.tile([PART, 2, 2, PART], F32, name="sums", tag="sums")
                for a in range(2):
                    for u in range(2):
                        turn(bank[:, u, a, :], u_raw[:, g, t0 + a, :], u)
                scale_out(
                    us_grouped[:, g, t0 : t0 + 2, :, :].rearrange("p a m x -> p (a m) x"),
                    bank[:].rearrange("p u a m -> p u (a m)"),
                    s_col[:],
                )

        def quantise_us(g):
            nc.vector.quantize_mx(
                out=us_codes[:, g, :].bitcast(E4M3_X4),
                scales=us_scales[:, g, :],
                in_=us_grouped[:, g].rearrange("p t m x -> p (t m x)"),
            )

        def multiply_us(g):
            for c in range(4):
                bank = psum.tile([PART, 4, PART], F32, name="sums", tag="sums")
                for t in range(4):
                    nc.tensor.matmul_mx(
                        out=bank[:, t, :],
                        lhsT=us_codes[:, g, t * PART : (t + 1) * PART].bitcast(E4M3_X4),
                        lhsT_scale=us_scales[:, g, t * PART : (t + 1) * PART],
                        rhs=v_words[:, 4 * PART * c : 4 * PART * (c + 1)].bitcast(E4M3_X4),
                        rhs_scale=v_scales[:, PART * c : PART * (c + 1)],
                        start=True,
                        stop=True,
                    )
                nc.scalar.copy(
                    out=p_grouped[:, g, PART * c : PART * (c + 1), :], in_=bank[:].rearrange("p t n -> p n t")
                )

        def quantise_p(g):
            nc.vector.quantize_mx(
                out=p_codes[:, g, :].bitcast(E4M3_X4),
                scales=p_scales[:, g, :],
                in_=p_grouped[:, g].rearrange("p n t -> p (n t)"),
            )


        def load(n):
            raw = stage.tile([PART, 4, HIDDEN], U8, name="raw", tag="raw", bufs=4)
            nc.sync.dma_start(out=raw[:], in_=h_rows[n])
            byte_tiles[n] = raw

        def widen(i):
            j = 2 * (i % 2)
            wide = stage.tile([PART, 2, HIDDEN], BF16, name="wide", tag="wide", bufs=WIDEN_AHEAD + 2)
            nc.scalar.copy(out=wide[:], in_=byte_tiles[i // 2][:, j : j + 2, :].bitcast(E4M3))
            wide_tiles[i] = wide

        def scale_tile0(i):
            product = stage.tile([PART, K_PASS], BF16, name="product", tag="product")
            nc.gpsimd.tensor_tensor(out=product[:], in0=wide_tiles[i][:, 0, K_PASS:], in1=scale_row[:], op=MULT)
            product_tiles[i] = product

        def turn_low(i):
            if i < FIRST_BY_SCALAR:
                bank = psum.tile([PART, 2, 2, PART], F32, name="low", tag="low", bufs=2)
                for a in range(2):
                    for u in range(2):
                        turn(bank[:, u, a, :], wide_tiles[i][:, a, 0:K_PASS], u)
            else:
                u = i % 2
                bank = psum.tile([PART, 4, PART], F32, name="low", tag="low", bufs=2)
                for j in range(4):
                    turn(bank[:, j, :], wide_tiles[i - u + j // 2][:, j % 2, 0:K_PASS], u)
            low_banks[i] = bank

        def turn_high(i):
            for a, rows in ((1, wide_tiles[i][:, 1, K_PASS:]), (0, product_tiles[i][:])):
                bank = psum.tile([PART, 2, PART], F32, name="high", tag="high")
                for u in range(2):
                    turn(bank[:, u, :], rows, u)
                high_banks[i, a] = bank

        def grouped_of(i):
            if i not in grouped_tiles:
                grouped = stage.tile(
                    [PART, 2, 2 * PART, 4], BF16, name="grouped", tag="grouped", bufs=6, align_bytes=64
                )
                grouped_tiles[i] = grouped
            return grouped_tiles[i]

        def scale_low_by_vector(i):
            scale_out(
                grouped_of(i)[:, 0, :, :], low_banks[i][:].rearrange("p u a r -> p u (a r)"), scale_col[:, 0, :]
            )

        def scale_low_by_scalar(i):
            u = i % 2
            if u == 0:
                halves = stage.tile([PART, 2, 4 * PART, 2], BF16, name="halves", tag="halves")
                half_tiles[i // 2] = halves
            words = low_banks[i][:].rearrange("p j r -> p (j r)").bitcast(BF16).rearrange("p (x e) -> p x e", e=2)
            for e in range(2):
                nc.scalar.activation(
                    out=half_tiles[i // 2][:, u, :, e],
                    in_=words[:, :, e],
                    func=COPY,
                    scale=scale_col[:, 0, 2 * u + e : 2 * u + e + 1],
                )

        def weave(i):
            words = half_tiles[i // 2][:].rearrange("p u x e -> p (u x e)").bitcast(F32)
            columns = slice(2 * PART * (i % 2), 2 * PART * (i % 2 + 1))
            nc.vector.tensor_copy(
                out=as_words(grouped_of(i)[:, 0, :, :]),
                in_=words.rearrange("p (u x) -> p x u", u=2)[:, columns, :],
            )

        def empty_high0(i, copy):
            copy(
                out=as_words(grouped_of(i)[:, 1, 0:PART, :]), in_=high_banks[i, 0][:].rearrange("p u r -> p r u")
            )

        def scale_high1(i):
            scale_out(grouped_of(i)[:, 1, PART:, :], high_banks[i, 1][:], scale_col[:, 1, :])

        def quantise(i):
            codes = quantised.tile([PART, 2, 2 * PART], U32, name="codes", align_bytes=64)
            scales = quantised.tile([PART, 2, 2 * PART], U8, name="scales", align_bytes=64)
            nc.vector.quantize_mx(
                out=codes[:].rearrange("p g x -> p (g x)").bitcast(E4M3_X4),
                scales=scales[:].rearrange("p g x -> p (g x)"),
                in_=grouped_tiles[i][:].rearrange("p g x t -> p (g x t)"),
            )
            code_tiles[i] = (codes, scales)

        def multiply(i, a):
            codes, scales = code_tiles[i]
            tokens = slice(PART * a, PART * (a + 1))
            bank = psum.tile([PART, OUT], F32, name="sums", tag="sums")
            for g in range(2):
                nc.tensor.matmul_mx(
                    out=bank[:],
                    lhsT=codes[:, g, tokens].bitcast(E4M3_X4),
                    lhsT_scale=scales[:, g, tokens],
                    rhs=p_codes[:, g, :].bitcast(E4M3_X4),
                    rhs_scale=p_scales[:, g, :],
                    start=(g == 0),
                    stop=(g == 1),
                )
            sum_banks[i, a] = bank

        def finish(i, a):
            if a == 0:
                result = stage.tile([PART, 2, OUT], F32, name="result", tag="result", bufs=5)
                result_tiles[i] = result
            result = result_tiles[i]
            nc.vector.tensor_tensor(out=result[:, a, :], in0=sum_banks[i, a][:], in1=bias_row[:], op=ADD)
            j = 2 * (i % 2)
            if i >= PAIRS - MULTIPLY_BEHIND:
                nc.sync.dma_start(out=out_rows[i // 2][:, j + a, :], in_=result[:, a, :])
            elif a == 1:
                nc.sync.dma_start(out=out_rows[i // 2][:, j : j + 2, :], in_=result[:])

        with tc.manual_schedule():
            nc.sync.dma_start(out=s_col[:], in_=c_proj_S.rearrange("(p t) -> p t", t=4))
            nc.sync.dma_start(out=scale_col[:], in_=h_scale.rearrange("a o (g p t) -> p (a o g) t", g=2, t=4))
            raw0 = stage.tile([PART, 4, HIDDEN], U8, name="raw", tag="raw", bufs=4)
            byte_tiles[0] = raw0
            nc.sync.dma_start(out=raw0[:, 0:2, :], in_=h_rows[0][:, 0:2, :])
            nc.sync.dma_start(out=u_raw[:, 0], in_=u_rows[0])
            nc.sync.dma_start(out=raw0[:, 2:4, :], in_=h_rows[0][:, 2:4, :])
            nc.sync.dma_start(out=u_raw[:, 1], in_=u_rows[1])
            load(1)
            nc.sync.dma_start(
                out=v_words[:].bitcast(I32), in_=c_proj_V_words[0].rearrange("p n t -> p (n t)").bitcast(I32)
            )
            for q in range(4):
                nc.sync.dma_start(
                    out=v_scales[32 * q : 32 * q + 4, :].bitcast(I32),
                    in_=c_proj_V_scales[0, 4 * q : 4 * q + 4, :].bitcast(I32),
                )
            load(2)
            nc.sync.dma_start(out=bias_col[:], in_=c_proj_bias.rearrange("(p t) -> p t", t=4))

            spread(scale_row, scale_col[:, 1, :])
            widen(0)
            turn_u(0)
            turn_low(0)
            scale_tile0(0)
            widen(1)
            widen(2)
            turn_high(0)
            quantise_us(0)
            widen(3)
            turn_u(1)
            scale_high1(0)
            scale_low_by_vector(0)
            empty_high0(0, nc.vector.tensor_copy)
            scale_tile0(1)
            multiply_us(0)
            quantise_us(1)

            for i in range(1, PAIRS):
                done = i - MULTIPLY_BEHIND
                if i % 2 == 1 and (i + 5) // 2 < QUADS:
                    load((i + 5) // 2)

                turn_low(i)
                if done >= 0:
                    multiply(done, 0)
                turn_high(i)
                if done >= 0:
                    multiply(done, 1)

                if i >= FIRST_BY_SCALAR:
                    scale_low_by_scalar(i)
                if i + WIDEN_AHEAD < PAIRS:
                    widen(i + WIDEN_AHEAD)
                if i >= FIRST_EMPTIED_BY_SCALAR:
                    empty_high0(i, nc.scalar.copy)

                if done >= 0:
                    finish(done, 0)
                scale_high1(i)
                if i >= QUANTISE_BEHIND:
                    quantise(i - QUANTISE_BEHIND)
                if i < FIRST_BY_SCALAR:
                    scale_low_by_vector(i)
                if i - WEAVE_BEHIND >= FIRST_BY_SCALAR:
                    weave(i - WEAVE_BEHIND)
                if i < FIRST_EMPTIED_BY_SCALAR:
                    empty_high0(i, nc.vector.tensor_copy)
                if done >= 0:
                    finish(done, 1)

                if i + 1 < PAIRS:
                    scale_tile0(i + 1)

                if i == 2:
                    nc.scalar.copy(out=bias_col_f32[:], in_=bias_col[:])
                    spread(bias_row, bias_col_f32[:])
                    quantise_p(0)
                    multiply_us(1)
                if i == 3:
                    quantise_p(1)

            last = PAIRS - 1
            weave(last - 1)
            quantise(last - 2)
            for i in range(PAIRS - MULTIPLY_BEHIND, PAIRS):
                if i == last - 3:
                    weave(last)
                if i == last - 2:
                    quantise(last - 1)
                if i == last - 1:
                    quantise(last)
                multiply(i, 0)
                multiply(i, 1)
                finish(i, 0)
                finish(i, 1)
